import numpy as np
import ml_dtypes


def mxq(x, axis, fmt="e4m3"):
    dtype, down = {"e4m3": (ml_dtypes.float8_e4m3fn, 7), "e5m2": (ml_dtypes.float8_e5m2, 14)}[fmt]
    v = np.moveaxis(np.asarray(x, np.float32).astype(ml_dtypes.bfloat16).astype(np.float64), axis, -1)
    blocks = v.reshape(v.shape[:-1] + (-1, 32))
    amax = np.abs(blocks).max(-1, keepdims=True)
    byte = np.maximum(np.where(amax > 0, np.frexp(amax)[1] - 1 + 127, 0) - down, 1)
    scale = np.exp2(byte - 127.0)
    codes = (blocks / scale).astype(np.float32).astype(dtype).astype(np.float64)
    return np.moveaxis((codes * scale).reshape(v.shape), -1, axis)


WIDE = False


def mx_kscale(k):
    if not WIDE:
        return np.ones(k)
    levels = np.array([10, -10, 5, -5, 0])
    if k % 512:
        return np.exp2(np.random.permutation(np.resize(levels, k // 32))).repeat(32)
    a = np.empty((k // 512, 16))
    for p in range(k // 512):
        a[p, :8] = np.random.permutation(np.resize(levels, 8))
        for g in range(8):
            far = levels[np.abs(levels - a[p, g]) >= 10]
            a[p, g + 8] = far[np.random.randint(len(far))]
    return np.exp2(a.ravel()).repeat(32)


BF16 = ml_dtypes.bfloat16


def bf(x):
    return np.asarray(x, np.float32).astype(BF16)


def f64(x):
    return np.asarray(x).astype(np.float64)


B, N, F, DIM, H, DH, D3 = 4, 196, 16, 512, 1, 64, 512
W = H * D3
SCALE = 1.0 / (np.sqrt(DH) * H)
QS = np.sqrt(1.5 / (SCALE * np.sqrt(D3)))


def draw0():
    s, t = mx_kscale(DIM), mx_kscale(D3)
    th = np.tile(t, H)
    return {"x": bf(np.random.standard_normal((B, N * F, DIM)) * s),
            "Wq": bf(np.random.standard_normal((DIM, W)) * QS / np.sqrt(DIM) / s[:, None] * th),
            "bq": bf(np.random.standard_normal(W) * 0.2 * QS * th),
            "k": bf(np.random.standard_normal((B, H, N, F, D3)) * QS / t)}


def core(x, Wq, bq, k):
    y = (mxq(f64(x), 2, "e4m3") @ mxq(f64(Wq), 0, "e4m3")) + f64(bq)
    q = y.reshape(B, F, N, H, D3).transpose(0, 3, 2, 1, 4)
    s = (mxq(q, 4, "e4m3") @ mxq(f64(k), 4, "e4m3").transpose(0, 1, 2, 4, 3)) * SCALE
    e = np.exp(s - s.max(-1, keepdims=True))
    return e / e.sum(-1, keepdims=True)


def e4m3fn_bytes(y):
    return np.clip(np.asarray(y, np.float64), -448.0, 448.0).astype(np.float32).astype(ml_dtypes.float8_e4m3fn).view(np.uint8)


def e4m3fn_values(b):
    return np.asarray(b, np.uint8).view(ml_dtypes.float8_e4m3fn).astype(np.float64)


def setup_inputs():
    d = draw0()
    x0 = np.asarray(d['x']).astype(np.float64)
    s = (np.max(np.abs(x0), axis=(0, 1), keepdims=True) / 448.0).astype(np.float32)
    out = {}
    for k, v in d.items():
        if k == 'x':
            out['x_bytes'] = e4m3fn_bytes(x0 / s.astype(np.float64))
            out['x_scale'] = s
        else:
            out[k] = v
    return out


def reference(x_bytes, x_scale, Wq, bq, k):
    return core(e4m3fn_values(x_bytes) * x_scale.astype(np.float64), Wq, bq, k)

@@ -1,0 +1,317 @@
+from contextlib import ExitStack
+
+import concourse.mybir as mybir
+from concourse.masks import make_identity
+
+F32 = mybir.dt.float32
+BF16 = mybir.dt.bfloat16
+U32 = mybir.dt.uint32
+U8 = mybir.dt.uint8
+FP8 = mybir.dt.float8_e4m3fn
+FP8X4 = mybir.dt.float8_e4m3fn_x4
+ALU = mybir.AluOpType
+ACT = mybir.ActivationFunctionType
+AXIS = mybir.AxisListType
+
+P = 128
+D = 512
+FRAMES = 16
+SETS = 8
+TILES = 98
+PAIR = 2
+BATCH = 8
+BANK = 512
+SOFTMAX_SCALE = 0.125
+
+FLOPS = 2 * TILES * P * D * D + 2 * TILES * P * FRAMES * D
+
+
+def tile_dividedspacetimeattention_pa_t_kernel(tc, x_bytes, x_scale, Wq, bq, k, out):
+    nc = tc.nc
+
+    groups = [(0, PAIR)] + [(r0, 2 * PAIR) for r0 in range(PAIR, TILES, 2 * PAIR)]
+    n_groups = len(groups)
+    place = [(0, 0)] + [((g + 1) // 2, 2 * PAIR * ((g + 1) % 2)) for g in range(1, n_groups)]
+    closes = {g: place[g][0] for g in range(0, n_groups, 2)}
+    batch_first = [0] + list(range(PAIR, TILES, BATCH))
+    batch_rows = [PAIR * FRAMES] + [P] * (len(batch_first) - 1)
+
+    x_rows = x_bytes.rearrange("b (q r) d -> (b q) (r d)", r=TILES)
+    k_rows = k.rearrange("b h (j r) g d -> r g (b h j) d", r=TILES)
+    out_rows = out.rearrange("b h (j r) f g -> (r f) (b h j) g", r=TILES)
+
+    with ExitStack() as ctx:
+        const = ctx.enter_context(tc.tile_pool(name="const", bufs=1))
+        loads = ctx.enter_context(tc.tile_pool(name="loads", bufs=1))
+        work = ctx.enter_context(tc.tile_pool(name="work", bufs=2))
+        psum = ctx.enter_context(tc.psum_pool(name="psum", bufs=1))
+        ctx.enter_context(tc.manual_schedule())
+
+        scale_col = const.tile([P, 4], F32, name="scale_col")
+        nc.sync.dma_start(out=scale_col[:], in_=x_scale.rearrange("a b (p t) -> p (a b t)", t=4))
+        xbytes = {}
+        kraw = {}
+
+        def load_x(g):
+            r0, n = groups[g]
+            xbytes[g] = loads.tile([P, n * D], U8, name="xbytes", tag="xbytes", bufs=n_groups, align_bytes=256)
+            nc.sync.dma_start(out=xbytes[g][:], in_=x_rows[:, r0 * D : (r0 + n) * D])
+
+        def load_k(g):
+            r0, n = groups[g]
+            for h in range(n // PAIR):
+                kraw[g, h] = loads.tile([P, PAIR * D], BF16, name="kraw", tag="kraw", bufs=TILES // PAIR, align_bytes=256)
+                for i in range(PAIR):
+                    nc.sync.dma_start(out=kraw[g, h][:, i * D : (i + 1) * D], in_=k_rows[r0 + PAIR * h + i])
+
+        load_x(0)
+        w_raw = const.tile([P, 4, D], BF16, name="w_raw", align_bytes=256)
+        nc.sync.dma_start(out=w_raw[:], in_=Wq.rearrange("(p j) c -> p j c", j=4))
+        bias = const.tile([P, 4], BF16, name="bias")
+        nc.sync.dma_start(out=bias[:], in_=bq.rearrange("(p t) -> p t", t=4))
+        load_x(1)
+        load_k(0)
+        for g in range(1, n_groups):
+            if g + 1 < n_groups:
+                load_x(g + 1)
+            load_k(g)
+
+        ident = const.tile([P, P], F32, name="ident")
+        make_identity(nc, ident[:])
+        x_order = const.tile([P, P], F32, name="x_order")
+        nc.vector.tensor_copy(
+            out=x_order[:].rearrange("p (b j f) -> p b j f", j=2, f=FRAMES),
+            in_=ident[:].rearrange("p (b f j) -> p b j f", j=2, f=FRAMES),
+        )
+        wrap = P - FRAMES
+        pick = const.tile([P, P + wrap], F32, name="pick")
+        ident_cg = ident[:].rearrange("p (g c) -> p c g", c=SETS)
+        nc.vector.tensor_copy(out=pick[:, :P].rearrange("p (c g) -> p c g", g=FRAMES), in_=ident_cg)
+        nc.vector.tensor_copy(out=pick[:, P:].rearrange("p (c g) -> p c g", g=FRAMES), in_=ident_cg[:, : SETS - 1, :])
+
+        def new_bank():
+            return psum.tile([P, BANK], F32, name="bank", tag="bank", bufs=7)
+
+        spread = new_bank()
+        for t in range(4):
+            nc.tensor.transpose(spread[:, t * P : (t + 1) * P], scale_col[:, t : t + 1].to_broadcast([P, P]), ident[:])
+        scales = const.tile([P, PAIR * D], F32, name="scales")
+        nc.vector.tensor_copy(
+            out=scales[:].rearrange("p (u r m e) -> p u r m e", u=2, r=PAIR, e=2),
+            in_=spread[:].rearrange("p (u e m) -> p u m e", u=2, e=2).unsqueeze(2).to_broadcast([P, 2, PAIR, P, 2]),
+        )
+
+        w_grouped = const.tile([P, 4 * D], BF16, name="w_grouped", align_bytes=64)
+        nc.scalar.copy(
+            out=w_grouped[:].rearrange("p (t m j) -> p t m j", t=4, j=4),
+            in_=w_raw[:].rearrange("p j (m t) -> p t m j", t=4),
+        )
+        w_codes = const.tile([P, D], U32, name="w_codes", align_bytes=64)
+        w_planes = const.tile([P, D], U8, name="w_planes", align_bytes=64)
+
+        scored = {}
+        scored[0] = work.tile([P, SETS * P], F32, name="scored", tag="scored")
+        nc.gpsimd.memset(scored[0][:].rearrange("p (c r f) -> p c r f", c=SETS, f=FRAMES)[:, :, PAIR:, :], 0.0)
+
+        xb, grouped, mx, planes, soft = {}, {}, {}, {}, {}
+
+        def pairs(g):
+            return groups[g][1] // PAIR
+
+        def widen(g, h):
+            if h >= pairs(g):
+                return
+            xb[g, h] = work.tile([P, PAIR * D], BF16, name="xb", tag="xb", bufs=4)
+            codes = xbytes[g][:, h * PAIR * D : (h + 1) * PAIR * D].bitcast(FP8)
+            nc.vector.tensor_tensor(
+                out=xb[g, h][:].rearrange("p (u q e) -> p u q e", u=2, e=2),
+                in0=codes.rearrange("p (q u e) -> p u q e", u=2, e=2),
+                in1=scales[:].rearrange("p (u q e) -> p u q e", u=2, e=2),
+                op=ALU.mult,
+            )
+
+        def empty_turned(which, g, h, bank):
+            if h == 0:
+                grouped[which, g] = work.tile(
+                    [P, groups[g][1] * D], BF16, name="grouped_" + which, tag="grouped_" + which, align_bytes=64
+                )
+            words = grouped[which, g][:, h * PAIR * D : (h + 1) * PAIR * D].bitcast(F32)
+            nc.scalar.copy(
+                out=words.rearrange("p (r n u) -> p r n u", r=PAIR, u=2),
+                in_=bank[:].rearrange("p (r u n) -> p r n u", r=PAIR, u=2),
+            )
+
+        def turn_x(g, h):
+            if h >= pairs(g):
+                return
+            bank = new_bank()
+            words = xb[g, h][:].bitcast(F32)
+            for r in range(PAIR):
+                for u in range(2):
+                    src = (u * PAIR + r) * P
+                    dst = (r * 2 + u) * P
+                    nc.tensor.transpose(bank[:, dst : dst + P], words[:, src : src + P], x_order[:])
+            empty_turned("x", g, h, bank)
+
+        def turn_k(g, h):
+            if h >= pairs(g):
+                return
+            bank = new_bank()
+            words = kraw[g, h][:].bitcast(F32)
+            for r in range(PAIR):
+                for u in range(2):
+                    dst = (r * 2 + u) * P
+                    nc.tensor.transpose(bank[:, dst : dst + P], words[:, r * 2 * P + u : (r + 1) * 2 * P : 2], ident[:])
+            empty_turned("k", g, h, bank)
+
+        def quantise(which, g):
+            width = groups[g][1] * P
+            codes = work.tile([P, width], U32, name="codes_" + which, tag="codes_" + which, align_bytes=64)
+            plane = work.tile([P, width], U8, name="plane_" + which, tag="plane_" + which, align_bytes=64)
+            nc.vector.quantize_mx(out=codes[:].bitcast(FP8X4), scales=plane[:], in_=grouped[which, g][:])
+            mx[which, g] = (codes, plane)
+
+        def project(g, t):
+            width = groups[g][1] * P
+            if t == 0:
+                planes[g] = work.tile([P, 4 * width], BF16, name="planes", tag="planes")
+            codes, plane = mx["x", g]
+            bank = new_bank()
+            nc.tensor.matmul_mx(
+                out=bank[:, :width],
+                lhsT=w_codes[:, t * P : (t + 1) * P].bitcast(FP8X4),
+                lhsT_scale=w_planes[:, t * P : (t + 1) * P],
+                rhs=codes[:].bitcast(FP8X4),
+                rhs_scale=plane[:],
+                start=True,
+                stop=True,
+            )
+            nc.scalar.activation(
+                out=planes[g][:, t * width : (t + 1) * width],
+                in_=bank[:, :width],
+                func=ACT.Identity,
+                bias=bias[:, t : t + 1],
+            )
+
+        def interleave(g):
+            width = groups[g][1] * P
+            grouped["q", g] = work.tile([P, 4 * width], BF16, name="grouped_q", tag="grouped_q", align_bytes=64)
+            nc.vector.tensor_copy(
+                out=grouped["q", g][:].rearrange("p (n t) -> p n t", t=4),
+                in_=planes[g][:].rearrange("p (t n) -> p n t", t=4),
+            )
+
+        def score(g):
+            n = groups[g][1]
+            batch, slot = place[g]
+            if batch not in scored:
+                scored[batch] = work.tile([P, SETS * P], F32, name="scored", tag="scored")
+            q_codes, q_plane = mx["q", g]
+            k_codes, k_plane = mx["k", g]
+            bank = new_bank()
+            for r in range(n):
+                cols = slice(r * P, (r + 1) * P)
+                nc.tensor.matmul_mx(
+                    out=bank[:, cols],
+                    lhsT=k_codes[:, cols].bitcast(FP8X4),
+                    lhsT_scale=k_plane[:, cols],
+                    rhs=q_codes[:, cols].bitcast(FP8X4),
+                    rhs_scale=q_plane[:, cols],
+                    start=True,
+                    stop=True,
+                )
+            nc.scalar.copy(
+                out=scored[batch][:].rearrange("p (c r f) -> p r c f", c=SETS, f=FRAMES)[:, slot : slot + n],
+                in_=bank[:, : n * P].rearrange("p (r c f) -> p r c f", c=SETS, f=FRAMES),
+            )
+
+        def cg(ap):
+            return ap.rearrange("p (c g) -> p c g", g=FRAMES)
+
+        def pick_scores(b):
+            picked = psum.tile([P, BANK], F32, name="picked", tag="picked")
+            for c in range(SETS):
+                window = slice(c * FRAMES, c * FRAMES + P)
+                nc.tensor.transpose(picked[:, window], scored[b][:, c * P : (c + 1) * P], pick[:, window])
+            soft[b, "picked"] = picked
+
+        def row_max(b):
+            rows = batch_rows[b]
+            top = work.tile([P, SETS], F32, name="top", tag="top")
+            nc.vector.tensor_reduce(out=top[:rows], in_=cg(soft[b, "picked"][:rows, :P]), axis=AXIS.X, op=ALU.max)
+            soft[b, "top"] = top
+
+        def shift(b):
+            rows = batch_rows[b]
+            shifted = work.tile([P, P], F32, name="shifted", tag="shifted")
+            nc.vector.tensor_tensor(
+                out=cg(shifted[:rows]),
+                in0=cg(soft[b, "picked"][:rows, :P]),
+                in1=soft[b, "top"][:rows].unsqueeze(2).to_broadcast([rows, SETS, FRAMES]),
+                op=ALU.subtract,
+            )
+            soft[b, "shifted"] = shifted
+
+        def exponent(b):
+            rows = batch_rows[b]
+            e = work.tile([P, P], F32, name="e", tag="e")
+            nc.scalar.activation(out=e[:rows], in_=soft[b, "shifted"][:rows], func=ACT.Exp, scale=SOFTMAX_SCALE)
+            soft[b, "e"] = e
+
+        def row_sum(b):
+            rows = batch_rows[b]
+            total = work.tile([P, SETS], F32, name="total", tag="total")
+            nc.vector.tensor_reduce(out=total[:rows], in_=cg(soft[b, "e"][:rows]), axis=AXIS.X, op=ALU.add)
+            soft[b, "total"] = total
+
+        def invert(b):
+            rows = batch_rows[b]
+            inverse = work.tile([P, SETS], F32, name="inverse", tag="inverse")
+            nc.vector.reciprocal(out=inverse[:rows], in_=soft[b, "total"][:rows])
+            soft[b, "inverse"] = inverse
+
+        def normalise(b):
+            rows = batch_rows[b]
+            weights = work.tile([P, P], F32, name="weights", tag="weights", bufs=len(batch_first))
+            nc.vector.tensor_tensor(
+                out=cg(weights[:rows]),
+                in0=cg(soft[b, "e"][:rows]),
+                in1=soft[b, "inverse"][:rows].unsqueeze(2).to_broadcast([rows, SETS, FRAMES]),
+                op=ALU.mult,
+            )
+            first = batch_first[b] * FRAMES
+            nc.sync.dma_start(out=out_rows[first : first + rows], in_=cg(weights[:rows]))
+
+        def on_group(fn, g, *args):
+            if 0 <= g < n_groups:
+                fn(g, *args)
+
+        def on_batch(fn, g):
+            if g in closes:
+                fn(closes[g])
+
+        for s in range(-2, n_groups + 3):
+            on_group(turn_x, s + 1, 0)
+            on_group(interleave, s - 1)
+            on_batch(row_sum, s - 3)
+            on_group(turn_x, s + 1, 1)
+            on_group(lambda g: quantise("k", g), s - 1)
+            on_batch(invert, s - 3)
+            on_group(project, s, 0)
+            on_group(project, s, 1)
+            on_group(widen, s + 2, 0)
+            on_batch(normalise, s - 3)
+            on_group(lambda g: quantise("q", g), s - 1)
+            on_group(turn_k, s, 0)
+            on_group(turn_k, s, 1)
+            on_batch(pick_scores, s - 2)
+            if s == -1:
+                nc.vector.quantize_mx(out=w_codes[:].bitcast(FP8X4), scales=w_planes[:], in_=w_grouped[:])
+            on_group(lambda g: quantise("x", g), s + 1)
+            on_batch(row_max, s - 2)
+            on_group(project, s, 2)
+            on_group(project, s, 3)
+            on_group(widen, s + 2, 1)
+            on_batch(shift, s - 2)
+            on_group(score, s - 1)
+            on_batch(exponent, s - 2)

@@ -21,6 +21,7 @@ TILES = 98
 PAIR = 2
 BATCH = 8
 BANK = 512
+AHEAD = 8
 SOFTMAX_SCALE = 0.125
 
 FLOPS = 2 * TILES * P * D * D + 2 * TILES * P * FRAMES * D
@@ -29,12 +30,14 @@ FLOPS = 2 * TILES * P * D * D + 2 * TILES * P * FRAMES * D
 def tile_dividedspacetimeattention_pa_t_kernel(tc, x_bytes, x_scale, Wq, bq, k, out):
     nc = tc.nc
 
-    groups = [(0, PAIR)] + [(r0, 2 * PAIR) for r0 in range(PAIR, TILES, 2 * PAIR)]
+    groups = [(0, PAIR)] + [(r0, 2 * PAIR) for r0 in range(PAIR, TILES - 2 * PAIR, 2 * PAIR)]
+    groups = groups + [(TILES - 2 * PAIR, PAIR), (TILES - PAIR, PAIR)]
     n_groups = len(groups)
-    place = [(0, 0)] + [((g + 1) // 2, 2 * PAIR * ((g + 1) % 2)) for g in range(1, n_groups)]
-    closes = {g: place[g][0] for g in range(0, n_groups, 2)}
     batch_first = [0] + list(range(PAIR, TILES, BATCH))
     batch_rows = [PAIR * FRAMES] + [P] * (len(batch_first) - 1)
+    batch_of = [max(b for b, first in enumerate(batch_first) if first <= r0) for r0, n in groups]
+    place = [(b, r0 - batch_first[b]) for b, (r0, n) in zip(batch_of, groups)]
+    closes = {g: b for g, b in enumerate(batch_of) if g + 1 == n_groups or batch_of[g + 1] != b}
 
     x_rows = x_bytes.rearrange("b (q r) d -> (b q) (r d)", r=TILES)
     k_rows = k.rearrange("b h (j r) g d -> r g (b h j) d", r=TILES)
@@ -54,13 +57,13 @@ def tile_dividedspacetimeattention_pa_t_kernel(tc, x_bytes, x_scale, Wq, bq, k, 
 
         def load_x(g):
             r0, n = groups[g]
-            xbytes[g] = loads.tile([P, n * D], U8, name="xbytes", tag="xbytes", bufs=n_groups, align_bytes=256)
+            xbytes[g] = loads.tile([P, n * D], U8, name="xbytes", tag="xbytes", bufs=AHEAD + 2, align_bytes=256)
             nc.sync.dma_start(out=xbytes[g][:], in_=x_rows[:, r0 * D : (r0 + n) * D])
 
         def load_k(g):
             r0, n = groups[g]
             for h in range(n // PAIR):
-                kraw[g, h] = loads.tile([P, PAIR * D], BF16, name="kraw", tag="kraw", bufs=TILES // PAIR, align_bytes=256)
+                kraw[g, h] = loads.tile([P, PAIR * D], BF16, name="kraw", tag="kraw", bufs=2 * AHEAD, align_bytes=256)
                 for i in range(PAIR):
                     nc.sync.dma_start(out=kraw[g, h][:, i * D : (i + 1) * D], in_=k_rows[r0 + PAIR * h + i])
 
@@ -69,11 +72,9 @@ def tile_dividedspacetimeattention_pa_t_kernel(tc, x_bytes, x_scale, Wq, bq, k, 
         nc.sync.dma_start(out=w_raw[:], in_=Wq.rearrange("(p j) c -> p j c", j=4))
         bias = const.tile([P, 4], BF16, name="bias")
         nc.sync.dma_start(out=bias[:], in_=bq.rearrange("(p t) -> p t", t=4))
-        load_x(1)
         load_k(0)
-        for g in range(1, n_groups):
-            if g + 1 < n_groups:
-                load_x(g + 1)
+        for g in range(1, AHEAD):
+            load_x(g)
             load_k(g)
 
         ident = const.tile([P, P], F32, name="ident")
@@ -90,16 +91,11 @@ def tile_dividedspacetimeattention_pa_t_kernel(tc, x_bytes, x_scale, Wq, bq, k, 
         nc.vector.tensor_copy(out=pick[:, P:].rearrange("p (c g) -> p c g", g=FRAMES), in_=ident_cg[:, : SETS - 1, :])
 
         def new_bank():
-            return psum.tile([P, BANK], F32, name="bank", tag="bank", bufs=7)
+            return psum.tile([P, BANK], F32, name="bank", tag="bank", bufs=6)
 
-        spread = new_bank()
+        scales = psum.tile([P, BANK], F32, name="scales", tag="scales")
         for t in range(4):
-            nc.tensor.transpose(spread[:, t * P : (t + 1) * P], scale_col[:, t : t + 1].to_broadcast([P, P]), ident[:])
-        scales = const.tile([P, PAIR * D], F32, name="scales")
-        nc.vector.tensor_copy(
-            out=scales[:].rearrange("p (u r m e) -> p u r m e", u=2, r=PAIR, e=2),
-            in_=spread[:].rearrange("p (u e m) -> p u m e", u=2, e=2).unsqueeze(2).to_broadcast([P, 2, PAIR, P, 2]),
-        )
+            nc.tensor.transpose(scales[:, t:BANK:4], scale_col[:, t : t + 1].to_broadcast([P, P]), ident[:])
 
         w_grouped = const.tile([P, 4 * D], BF16, name="w_grouped", align_bytes=64)
         nc.scalar.copy(
@@ -122,13 +118,14 @@ def tile_dividedspacetimeattention_pa_t_kernel(tc, x_bytes, x_scale, Wq, bq, k, 
             if h >= pairs(g):
                 return
             xb[g, h] = work.tile([P, PAIR * D], BF16, name="xb", tag="xb", bufs=4)
-            codes = xbytes[g][:, h * PAIR * D : (h + 1) * PAIR * D].bitcast(FP8)
-            nc.vector.tensor_tensor(
-                out=xb[g, h][:].rearrange("p (u q e) -> p u q e", u=2, e=2),
-                in0=codes.rearrange("p (q u e) -> p u q e", u=2, e=2),
-                in1=scales[:].rearrange("p (u q e) -> p u q e", u=2, e=2),
-                op=ALU.mult,
-            )
+            for r in range(PAIR):
+                first = (h * PAIR + r) * D
+                nc.vector.tensor_tensor(
+                    out=xb[g, h][:, r * D : (r + 1) * D],
+                    in0=xbytes[g][:, first : first + D].bitcast(FP8),
+                    in1=scales[:],
+                    op=ALU.mult,
+                )
 
         def empty_turned(which, g, h, bank):
             if h == 0:
@@ -148,9 +145,8 @@ def tile_dividedspacetimeattention_pa_t_kernel(tc, x_bytes, x_scale, Wq, bq, k, 
             words = xb[g, h][:].bitcast(F32)
             for r in range(PAIR):
                 for u in range(2):
-                    src = (u * PAIR + r) * P
                     dst = (r * 2 + u) * P
-                    nc.tensor.transpose(bank[:, dst : dst + P], words[:, src : src + P], x_order[:])
+                    nc.tensor.transpose(bank[:, dst : dst + P], words[:, r * 2 * P + u : (r + 1) * 2 * P : 2], x_order[:])
             empty_turned("x", g, h, bank)
 
         def turn_k(g, h):
@@ -166,15 +162,16 @@ def tile_dividedspacetimeattention_pa_t_kernel(tc, x_bytes, x_scale, Wq, bq, k, 
 
         def quantise(which, g):
             width = groups[g][1] * P
-            codes = work.tile([P, width], U32, name="codes_" + which, tag="codes_" + which, align_bytes=64)
-            plane = work.tile([P, width], U8, name="plane_" + which, tag="plane_" + which, align_bytes=64)
+            depth = 4 if which == "k" else 2
+            codes = work.tile([P, width], U32, name="codes_" + which, tag="codes_" + which, bufs=depth, align_bytes=64)
+            plane = work.tile([P, width], U8, name="plane_" + which, tag="plane_" + which, bufs=depth, align_bytes=64)
             nc.vector.quantize_mx(out=codes[:].bitcast(FP8X4), scales=plane[:], in_=grouped[which, g][:])
             mx[which, g] = (codes, plane)
 
         def project(g, t):
             width = groups[g][1] * P
             if t == 0:
-                planes[g] = work.tile([P, 4 * width], BF16, name="planes", tag="planes")
+                planes[g] = work.tile([P, 4 * width], BF16, name="planes", tag="planes", bufs=3)
             codes, plane = mx["x", g]
             bank = new_bank()
             nc.tensor.matmul_mx(
@@ -195,11 +192,13 @@ def tile_dividedspacetimeattention_pa_t_kernel(tc, x_bytes, x_scale, Wq, bq, k, 
 
         def interleave(g):
             width = groups[g][1] * P
-            grouped["q", g] = work.tile([P, 4 * width], BF16, name="grouped_q", tag="grouped_q", align_bytes=64)
-            nc.vector.tensor_copy(
-                out=grouped["q", g][:].rearrange("p (n t) -> p n t", t=4),
-                in_=planes[g][:].rearrange("p (t n) -> p n t", t=4),
-            )
+            grouped["q", g] = work.tile([P, 4 * width], BF16, name="grouped_q", tag="grouped_q", bufs=1, align_bytes=64)
+            dst = grouped["q", g][:].rearrange("p (n t) -> p n t", t=4)
+            src = planes[g][:].rearrange("p (t n) -> p n t", t=4)
+            if g + 4 < n_groups:
+                nc.gpsimd.tensor_scalar(out=dst, in0=src, scalar1=1.0, scalar2=0.0, op0=ALU.mult, op1=ALU.add)
+            else:
+                nc.vector.tensor_copy(out=dst, in_=src)
 
         def score(g):
             n = groups[g][1]
@@ -220,7 +219,13 @@ def tile_dividedspacetimeattention_pa_t_kernel(tc, x_bytes, x_scale, Wq, bq, k, 
                     start=True,
                     stop=True,
                 )
-            nc.scalar.copy(
+            soft[g, "bank"] = bank
+
+        def empty_scores(g):
+            n = groups[g][1]
+            batch, slot = place[g]
+            bank = soft[g, "bank"]
+            nc.vector.tensor_copy(
                 out=scored[batch][:].rearrange("p (c r f) -> p r c f", c=SETS, f=FRAMES)[:, slot : slot + n],
                 in_=bank[:, : n * P].rearrange("p (r c f) -> p r c f", c=SETS, f=FRAMES),
             )
@@ -290,28 +295,32 @@ def tile_dividedspacetimeattention_pa_t_kernel(tc, x_bytes, x_scale, Wq, bq, k, 
             if g in closes:
                 fn(closes[g])
 
-        for s in range(-2, n_groups + 3):
-            on_group(turn_x, s + 1, 0)
-            on_group(interleave, s - 1)
-            on_batch(row_sum, s - 3)
-            on_group(turn_x, s + 1, 1)
-            on_group(lambda g: quantise("k", g), s - 1)
-            on_batch(invert, s - 3)
+        for s in range(-3, n_groups + 5):
+            on_group(lambda g: quantise("x", g), s + 1)
             on_group(project, s, 0)
             on_group(project, s, 1)
-            on_group(widen, s + 2, 0)
-            on_batch(normalise, s - 3)
-            on_group(lambda g: quantise("q", g), s - 1)
-            on_group(turn_k, s, 0)
-            on_group(turn_k, s, 1)
-            on_batch(pick_scores, s - 2)
+            on_batch(exponent, s - 4)
+            on_group(lambda g: quantise("k", g), s + 1)
             if s == -1:
                 nc.vector.quantize_mx(out=w_codes[:].bitcast(FP8X4), scales=w_planes[:], in_=w_grouped[:])
-            on_group(lambda g: quantise("x", g), s + 1)
-            on_batch(row_max, s - 2)
+            on_batch(normalise, s - 5)
+            on_group(lambda g: quantise("q", g), s - 2)
+            on_group(turn_x, s + 2, 0)
+            on_group(turn_x, s + 2, 1)
             on_group(project, s, 2)
             on_group(project, s, 3)
-            on_group(widen, s + 2, 1)
-            on_batch(shift, s - 2)
-            on_group(score, s - 1)
-            on_batch(exponent, s - 2)
+            on_group(turn_k, s + 2, 0)
+            on_group(turn_k, s + 2, 1)
+            on_batch(pick_scores, s - 3)
+            on_group(score, s - 2)
+            on_group(interleave, s - 1)
+            on_group(widen, s + 3, 0)
+            on_batch(row_max, s - 3)
+            on_batch(row_sum, s - 4)
+            on_group(widen, s + 3, 1)
+            on_batch(shift, s - 3)
+            on_batch(invert, s - 4)
+            on_group(empty_scores, s - 2)
+            if s + 2 >= 0:
+                on_group(load_x, s + 2 + AHEAD)
+                on_group(load_k, s + 2 + AHEAD)

@@ -15,13 +15,17 @@ AXIS = mybir.AxisListType
 
 P = 128
 D = 512
+PACK = 4
 FRAMES = 16
 SETS = 8
 TILES = 98
-PAIR = 2
-BATCH = 8
 BANK = 512
+PAIR = 2
+GROUP = 4
+BATCH = P // FRAMES
+RING = 6
 AHEAD = 8
+TAIL = 4
 SOFTMAX_SCALE = 0.125
 
 FLOPS = 2 * TILES * P * D * D + 2 * TILES * P * FRAMES * D
@@ -30,14 +34,13 @@ FLOPS = 2 * TILES * P * D * D + 2 * TILES * P * FRAMES * D
 def tile_dividedspacetimeattention_pa_t_kernel(tc, x_bytes, x_scale, Wq, bq, k, out):
     nc = tc.nc
 
-    groups = [(0, PAIR)] + [(r0, 2 * PAIR) for r0 in range(PAIR, TILES - 2 * PAIR, 2 * PAIR)]
-    groups = groups + [(TILES - 2 * PAIR, PAIR), (TILES - PAIR, PAIR)]
+    groups = [(0, PAIR)] + [(r0, GROUP) for r0 in range(PAIR, TILES - GROUP, GROUP)]
+    groups = groups + [(TILES - GROUP, PAIR), (TILES - PAIR, PAIR)]
     n_groups = len(groups)
     batch_first = [0] + list(range(PAIR, TILES, BATCH))
     batch_rows = [PAIR * FRAMES] + [P] * (len(batch_first) - 1)
     batch_of = [max(b for b, first in enumerate(batch_first) if first <= r0) for r0, n in groups]
-    place = [(b, r0 - batch_first[b]) for b, (r0, n) in zip(batch_of, groups)]
-    closes = {g: b for g, b in enumerate(batch_of) if g + 1 == n_groups or batch_of[g + 1] != b}
+    batch_closed_by = {g: b for g, b in enumerate(batch_of) if g + 1 == n_groups or batch_of[g + 1] != b}
 
     x_rows = x_bytes.rearrange("b (q r) d -> (b q) (r d)", r=TILES)
     k_rows = k.rearrange("b h (j r) g d -> r g (b h j) d", r=TILES)
@@ -50,10 +53,7 @@ def tile_dividedspacetimeattention_pa_t_kernel(tc, x_bytes, x_scale, Wq, bq, k, 
         psum = ctx.enter_context(tc.psum_pool(name="psum", bufs=1))
         ctx.enter_context(tc.manual_schedule())
 
-        scale_col = const.tile([P, 4], F32, name="scale_col")
-        nc.sync.dma_start(out=scale_col[:], in_=x_scale.rearrange("a b (p t) -> p (a b t)", t=4))
-        xbytes = {}
-        kraw = {}
+        xbytes, kraw, widened, joint, planes, q_words, mx, score_bank, scored, soft = [{} for i in range(10)]
 
         def load_x(g):
             r0, n = groups[g]
@@ -67,15 +67,24 @@ def tile_dividedspacetimeattention_pa_t_kernel(tc, x_bytes, x_scale, Wq, bq, k, 
                 for i in range(PAIR):
                     nc.sync.dma_start(out=kraw[g, h][:, i * D : (i + 1) * D], in_=k_rows[r0 + PAIR * h + i])
 
-        load_x(0)
-        w_raw = const.tile([P, 4, D], BF16, name="w_raw", align_bytes=256)
-        nc.sync.dma_start(out=w_raw[:], in_=Wq.rearrange("(p j) c -> p j c", j=4))
-        bias = const.tile([P, 4], BF16, name="bias")
-        nc.sync.dma_start(out=bias[:], in_=bq.rearrange("(p t) -> p t", t=4))
-        load_k(0)
-        for g in range(1, AHEAD):
+        scale_col = const.tile([P, PACK], F32, name="scale_col")
+        nc.sync.dma_start(out=scale_col[:], in_=x_scale.rearrange("a b (p t) -> p (a b t)", t=PACK))
+        for g in range(2):
             load_x(g)
             load_k(g)
+        w_raw = const.tile([P, PACK, D], BF16, name="w_raw", align_bytes=256)
+        nc.sync.dma_start(out=w_raw[:], in_=Wq.rearrange("(p j) c -> p j c", j=PACK))
+        bias = const.tile([P, PACK], BF16, name="bias")
+        nc.sync.dma_start(out=bias[:], in_=bq.rearrange("(p t) -> p t", t=PACK))
+        for g in range(2, AHEAD):
+            load_x(g)
+            load_k(g)
+
+        def new_scored(b):
+            scored[b] = work.tile([P, SETS * P], F32, name="scored", tag="scored")
+
+        new_scored(0)
+        nc.vector.memset(scored[0][:].rearrange("p (c r f) -> p c r f", c=SETS, f=FRAMES)[:, :, PAIR:, :], 0.0)
 
         ident = const.tile([P, P], F32, name="ident")
         make_identity(nc, ident[:])
@@ -84,102 +93,88 @@ def tile_dividedspacetimeattention_pa_t_kernel(tc, x_bytes, x_scale, Wq, bq, k, 
             out=x_order[:].rearrange("p (b j f) -> p b j f", j=2, f=FRAMES),
             in_=ident[:].rearrange("p (b f j) -> p b j f", j=2, f=FRAMES),
         )
-        wrap = P - FRAMES
-        pick = const.tile([P, P + wrap], F32, name="pick")
+        pick = const.tile([P, 2 * P - FRAMES], F32, name="pick")
         ident_cg = ident[:].rearrange("p (g c) -> p c g", c=SETS)
         nc.vector.tensor_copy(out=pick[:, :P].rearrange("p (c g) -> p c g", g=FRAMES), in_=ident_cg)
         nc.vector.tensor_copy(out=pick[:, P:].rearrange("p (c g) -> p c g", g=FRAMES), in_=ident_cg[:, : SETS - 1, :])
 
-        def new_bank():
-            return psum.tile([P, BANK], F32, name="bank", tag="bank", bufs=6)
-
         scales = psum.tile([P, BANK], F32, name="scales", tag="scales")
-        for t in range(4):
-            nc.tensor.transpose(scales[:, t:BANK:4], scale_col[:, t : t + 1].to_broadcast([P, P]), ident[:])
+        for t in range(PACK):
+            nc.tensor.transpose(scales[:, t:BANK:PACK], scale_col[:, t : t + 1].to_broadcast([P, P]), ident[:])
 
-        w_grouped = const.tile([P, 4 * D], BF16, name="w_grouped", align_bytes=64)
-        nc.scalar.copy(
-            out=w_grouped[:].rearrange("p (t m j) -> p t m j", t=4, j=4),
-            in_=w_raw[:].rearrange("p j (m t) -> p t m j", t=4),
+        def gpsimd_copy(dst, src):
+            nc.gpsimd.tensor_scalar(out=dst, in0=src, scalar1=1.0, scalar2=0.0, op0=ALU.mult, op1=ALU.add)
+
+        w_words = const.tile([P, PACK * D], BF16, name="w_words", align_bytes=64)
+        gpsimd_copy(
+            w_words[:].rearrange("p (t m j) -> p t m j", t=PACK, j=PACK),
+            w_raw[:].rearrange("p j (m t) -> p t m j", t=PACK),
         )
         w_codes = const.tile([P, D], U32, name="w_codes", align_bytes=64)
-        w_planes = const.tile([P, D], U8, name="w_planes", align_bytes=64)
+        w_scales = const.tile([P, D], U8, name="w_scales", align_bytes=64)
 
-        scored = {}
-        scored[0] = work.tile([P, SETS * P], F32, name="scored", tag="scored")
-        nc.gpsimd.memset(scored[0][:].rearrange("p (c r f) -> p c r f", c=SETS, f=FRAMES)[:, :, PAIR:, :], 0.0)
+        def new_bank():
+            return psum.tile([P, BANK], F32, name="bank", tag="bank", bufs=RING)
 
-        xb, grouped, mx, planes, soft = {}, {}, {}, {}, {}
-
-        def pairs(g):
-            return groups[g][1] // PAIR
+        def quantise(codes, block_scales, values):
+            nc.vector.quantize_mx(out=codes.bitcast(FP8X4), scales=block_scales, in_=values)
 
         def widen(g, h):
-            if h >= pairs(g):
-                return
-            xb[g, h] = work.tile([P, PAIR * D], BF16, name="xb", tag="xb", bufs=4)
+            widened[g, h] = work.tile([P, PAIR * D], BF16, name="widened", tag="widened", bufs=4)
             for r in range(PAIR):
                 first = (h * PAIR + r) * D
                 nc.vector.tensor_tensor(
-                    out=xb[g, h][:, r * D : (r + 1) * D],
+                    out=widened[g, h][:, r * D : (r + 1) * D],
                     in0=xbytes[g][:, first : first + D].bitcast(FP8),
                     in1=scales[:],
                     op=ALU.mult,
                 )
 
-        def empty_turned(which, g, h, bank):
-            if h == 0:
-                grouped[which, g] = work.tile(
-                    [P, groups[g][1] * D], BF16, name="grouped_" + which, tag="grouped_" + which, align_bytes=64
-                )
-            words = grouped[which, g][:, h * PAIR * D : (h + 1) * PAIR * D].bitcast(F32)
+        def turn(rows, order, step, first):
+            bank = new_bank()
+            words = rows[:].bitcast(F32)
+            for r in range(PAIR):
+                for u in range(2):
+                    slot = (r * 2 + u) * P
+                    nc.tensor.transpose(bank[:, slot : slot + P], words[:, r * 2 * P + u : (r + 1) * 2 * P : 2], order[:])
+            if step not in joint:
+                joint[step] = work.tile([P, 2 * GROUP * D], BF16, name="joint", tag="joint", bufs=5, align_bytes=64)
             nc.scalar.copy(
-                out=words.rearrange("p (r n u) -> p r n u", r=PAIR, u=2),
+                out=joint[step][:, first : first + PAIR * D].bitcast(F32).rearrange("p (r n u) -> p r n u", r=PAIR, u=2),
                 in_=bank[:].rearrange("p (r u n) -> p r n u", r=PAIR, u=2),
             )
 
         def turn_x(g, h):
-            if h >= pairs(g):
-                return
-            bank = new_bank()
-            words = xb[g, h][:].bitcast(F32)
-            for r in range(PAIR):
-                for u in range(2):
-                    dst = (r * 2 + u) * P
-                    nc.tensor.transpose(bank[:, dst : dst + P], words[:, r * 2 * P + u : (r + 1) * 2 * P : 2], x_order[:])
-            empty_turned("x", g, h, bank)
+            turn(widened[g, h], x_order, g - 1, h * PAIR * D)
 
         def turn_k(g, h):
-            if h >= pairs(g):
-                return
-            bank = new_bank()
-            words = kraw[g, h][:].bitcast(F32)
-            for r in range(PAIR):
-                for u in range(2):
-                    dst = (r * 2 + u) * P
-                    nc.tensor.transpose(bank[:, dst : dst + P], words[:, r * 2 * P + u : (r + 1) * 2 * P : 2], ident[:])
-            empty_turned("k", g, h, bank)
+            turn(kraw[g, h], ident, g + 1, (GROUP + h * PAIR) * D)
 
-        def quantise(which, g):
-            width = groups[g][1] * P
-            depth = 4 if which == "k" else 2
-            codes = work.tile([P, width], U32, name="codes_" + which, tag="codes_" + which, bufs=depth, align_bytes=64)
-            plane = work.tile([P, width], U8, name="plane_" + which, tag="plane_" + which, bufs=depth, align_bytes=64)
-            nc.vector.quantize_mx(out=codes[:].bitcast(FP8X4), scales=plane[:], in_=grouped[which, g][:])
-            mx[which, g] = (codes, plane)
+        def quantise_x_and_k(step):
+            codes = work.tile([P, 2 * BANK], U32, name="xk_codes", tag="xk_codes", align_bytes=64)
+            block_scales = work.tile([P, 2 * BANK], U8, name="xk_scales", tag="xk_scales", align_bytes=64)
+            parts = [("x", step + 1, 0), ("k", step - 1, BANK)]
+            parts = [(name, g, slice(c0, c0 + groups[g][1] * P)) for name, g, c0 in parts if 0 <= g < n_groups]
+            for name, g, cols in parts:
+                mx[name, g] = (codes[:, cols], block_scales[:, cols])
+            if sum(cols.stop - cols.start for name, g, cols in parts) == 2 * BANK:
+                quantise(codes[:], block_scales[:], joint[step][:])
+            else:
+                for name, g, cols in parts:
+                    quantise(codes[:, cols], block_scales[:, cols], joint[step][:, PACK * cols.start : PACK * cols.stop])
 
         def project(g, t):
             width = groups[g][1] * P
             if t == 0:
-                planes[g] = work.tile([P, 4 * width], BF16, name="planes", tag="planes", bufs=3)
-            codes, plane = mx["x", g]
+                planes[g] = work.tile([P, PACK * width], BF16, name="planes", tag="planes", bufs=3)
+            x_codes, x_scales = mx["x", g]
             bank = new_bank()
             nc.tensor.matmul_mx(
                 out=bank[:, :width],
                 lhsT=w_codes[:, t * P : (t + 1) * P].bitcast(FP8X4),
-                lhsT_scale=w_planes[:, t * P : (t + 1) * P],
-                rhs=codes[:].bitcast(FP8X4),
-                rhs_scale=plane[:],
+                lhsT_scale=w_scales[:, t * P : (t + 1) * P],
+                rhs=x_codes.bitcast(FP8X4),
+                rhs_scale=x_scales,
                 start=True,
                 stop=True,
             )
@@ -192,45 +187,53 @@ def tile_dividedspacetimeattention_pa_t_kernel(tc, x_bytes, x_scale, Wq, bq, k, 
 
         def interleave(g):
             width = groups[g][1] * P
-            grouped["q", g] = work.tile([P, 4 * width], BF16, name="grouped_q", tag="grouped_q", bufs=1, align_bytes=64)
-            dst = grouped["q", g][:].rearrange("p (n t) -> p n t", t=4)
-            src = planes[g][:].rearrange("p (t n) -> p n t", t=4)
-            if g + 4 < n_groups:
-                nc.gpsimd.tensor_scalar(out=dst, in0=src, scalar1=1.0, scalar2=0.0, op0=ALU.mult, op1=ALU.add)
+            src = planes[g][:].rearrange("p (t n) -> p n t", t=PACK)
+            if g + TAIL < n_groups:
+                q_words[g] = work.tile([P, PACK * width], BF16, name="q_words", tag="q_words", bufs=1, align_bytes=64)
+                gpsimd_copy(q_words[g][:].rearrange("p (n t) -> p n t", t=PACK), src)
             else:
-                nc.vector.tensor_copy(out=dst, in_=src)
+                q_words[g] = work.tile([P, PACK * width], BF16, name="q_words_tail", tag="q_words_tail", align_bytes=64)
+                dst = q_words[g][:].rearrange("p (n t) -> p n t", t=PACK)
+                nc.scalar.copy(out=dst[:, : width // 2], in_=src[:, : width // 2])
+                nc.vector.tensor_copy(out=dst[:, width // 2 :], in_=src[:, width // 2 :])
+
+        def quantise_q(g):
+            width = groups[g][1] * P
+            codes = work.tile([P, width], U32, name="q_codes", tag="q_codes", align_bytes=64)
+            block_scales = work.tile([P, width], U8, name="q_scales", tag="q_scales", align_bytes=64)
+            quantise(codes[:], block_scales[:], q_words[g][:])
+            mx["q", g] = (codes[:], block_scales[:])
 
         def score(g):
-            n = groups[g][1]
-            batch, slot = place[g]
-            if batch not in scored:
-                scored[batch] = work.tile([P, SETS * P], F32, name="scored", tag="scored")
-            q_codes, q_plane = mx["q", g]
-            k_codes, k_plane = mx["k", g]
-            bank = new_bank()
-            for r in range(n):
+            q_codes, q_scales = mx["q", g]
+            k_codes, k_scales = mx["k", g]
+            score_bank[g] = new_bank()
+            for r in range(groups[g][1]):
                 cols = slice(r * P, (r + 1) * P)
                 nc.tensor.matmul_mx(
-                    out=bank[:, cols],
+                    out=score_bank[g][:, cols],
                     lhsT=k_codes[:, cols].bitcast(FP8X4),
-                    lhsT_scale=k_plane[:, cols],
+                    lhsT_scale=k_scales[:, cols],
                     rhs=q_codes[:, cols].bitcast(FP8X4),
-                    rhs_scale=q_plane[:, cols],
+                    rhs_scale=q_scales[:, cols],
                     start=True,
                     stop=True,
                 )
-            soft[g, "bank"] = bank
 
         def empty_scores(g):
-            n = groups[g][1]
-            batch, slot = place[g]
-            bank = soft[g, "bank"]
-            nc.vector.tensor_copy(
-                out=scored[batch][:].rearrange("p (c r f) -> p r c f", c=SETS, f=FRAMES)[:, slot : slot + n],
-                in_=bank[:, : n * P].rearrange("p (r c f) -> p r c f", c=SETS, f=FRAMES),
-            )
+            r0, n = groups[g]
+            b = batch_of[g]
+            if b not in scored:
+                new_scored(b)
+            slot = r0 - batch_first[b]
+            dst = scored[b][:].rearrange("p (c r f) -> p r c f", c=SETS, f=FRAMES)[:, slot : slot + n]
+            src = score_bank[g][:, : n * P].rearrange("p (r c f) -> p r c f", c=SETS, f=FRAMES)
+            if g % 2 == 0:
+                nc.vector.tensor_copy(out=dst, in_=src)
+            else:
+                nc.scalar.copy(out=dst, in_=src)
 
-        def cg(ap):
+        def by_set(ap):
             return ap.rearrange("p (c g) -> p c g", g=FRAMES)
 
         def pick_scores(b):
@@ -238,89 +241,84 @@ def tile_dividedspacetimeattention_pa_t_kernel(tc, x_bytes, x_scale, Wq, bq, k, 
             for c in range(SETS):
                 window = slice(c * FRAMES, c * FRAMES + P)
                 nc.tensor.transpose(picked[:, window], scored[b][:, c * P : (c + 1) * P], pick[:, window])
-            soft[b, "picked"] = picked
+            soft[b, "picked"] = by_set(picked[: batch_rows[b], :P])
+
+        def per_set(ap, b):
+            return ap.unsqueeze(2).to_broadcast([batch_rows[b], SETS, FRAMES])
 
         def row_max(b):
-            rows = batch_rows[b]
             top = work.tile([P, SETS], F32, name="top", tag="top")
-            nc.vector.tensor_reduce(out=top[:rows], in_=cg(soft[b, "picked"][:rows, :P]), axis=AXIS.X, op=ALU.max)
-            soft[b, "top"] = top
+            soft[b, "top"] = top[: batch_rows[b]]
+            nc.vector.tensor_reduce(out=soft[b, "top"], in_=soft[b, "picked"], axis=AXIS.X, op=ALU.max)
 
         def shift(b):
-            rows = batch_rows[b]
             shifted = work.tile([P, P], F32, name="shifted", tag="shifted")
+            soft[b, "shifted"] = shifted[: batch_rows[b]]
             nc.vector.tensor_tensor(
-                out=cg(shifted[:rows]),
-                in0=cg(soft[b, "picked"][:rows, :P]),
-                in1=soft[b, "top"][:rows].unsqueeze(2).to_broadcast([rows, SETS, FRAMES]),
-                op=ALU.subtract,
+                out=by_set(soft[b, "shifted"]), in0=soft[b, "picked"], in1=per_set(soft[b, "top"], b), op=ALU.subtract
             )
-            soft[b, "shifted"] = shifted
 
         def exponent(b):
-            rows = batch_rows[b]
-            e = work.tile([P, P], F32, name="e", tag="e")
-            nc.scalar.activation(out=e[:rows], in_=soft[b, "shifted"][:rows], func=ACT.Exp, scale=SOFTMAX_SCALE)
-            soft[b, "e"] = e
+            powers = work.tile([P, P], F32, name="powers", tag="powers")
+            soft[b, "powers"] = powers[: batch_rows[b]]
+            nc.scalar.activation(out=soft[b, "powers"], in_=soft[b, "shifted"], func=ACT.Exp, scale=SOFTMAX_SCALE)
 
         def row_sum(b):
-            rows = batch_rows[b]
             total = work.tile([P, SETS], F32, name="total", tag="total")
-            nc.vector.tensor_reduce(out=total[:rows], in_=cg(soft[b, "e"][:rows]), axis=AXIS.X, op=ALU.add)
-            soft[b, "total"] = total
+            soft[b, "total"] = total[: batch_rows[b]]
+            nc.vector.tensor_reduce(out=soft[b, "total"], in_=by_set(soft[b, "powers"]), axis=AXIS.X, op=ALU.add)
 
         def invert(b):
-            rows = batch_rows[b]
             inverse = work.tile([P, SETS], F32, name="inverse", tag="inverse")
-            nc.vector.reciprocal(out=inverse[:rows], in_=soft[b, "total"][:rows])
-            soft[b, "inverse"] = inverse
+            soft[b, "inverse"] = inverse[: batch_rows[b]]
+            nc.vector.reciprocal(out=soft[b, "inverse"], in_=soft[b, "total"])
 
         def normalise(b):
-            rows = batch_rows[b]
-            weights = work.tile([P, P], F32, name="weights", tag="weights", bufs=len(batch_first))
-            nc.vector.tensor_tensor(
-                out=cg(weights[:rows]),
-                in0=cg(soft[b, "e"][:rows]),
-                in1=soft[b, "inverse"][:rows].unsqueeze(2).to_broadcast([rows, SETS, FRAMES]),
-                op=ALU.mult,
-            )
+            weights = work.tile([P, P], F32, name="weights", tag="weights")
+            rows = by_set(weights[: batch_rows[b]])
+            nc.vector.tensor_tensor(out=rows, in0=by_set(soft[b, "powers"]), in1=per_set(soft[b, "inverse"], b), op=ALU.mult)
             first = batch_first[b] * FRAMES
-            nc.sync.dma_start(out=out_rows[first : first + rows], in_=cg(weights[:rows]))
+            nc.sync.dma_start(out=out_rows[first : first + batch_rows[b]], in_=rows)
 
         def on_group(fn, g, *args):
             if 0 <= g < n_groups:
                 fn(g, *args)
 
-        def on_batch(fn, g):
-            if g in closes:
-                fn(closes[g])
+        def on_pair(fn, g, h):
+            if 0 <= g < n_groups and h * PAIR < groups[g][1]:
+                fn(g, h)
 
-        for s in range(-3, n_groups + 5):
-            on_group(lambda g: quantise("x", g), s + 1)
+        def on_batch(fn, g):
+            if g in batch_closed_by:
+                fn(batch_closed_by[g])
+
+        first_step = -3
+        for s in range(first_step, n_groups + 6):
+            if s >= 0 and s in joint:
+                quantise_x_and_k(s)
             on_group(project, s, 0)
             on_group(project, s, 1)
             on_batch(exponent, s - 4)
-            on_group(lambda g: quantise("k", g), s + 1)
-            if s == -1:
-                nc.vector.quantize_mx(out=w_codes[:].bitcast(FP8X4), scales=w_planes[:], in_=w_grouped[:])
-            on_batch(normalise, s - 5)
-            on_group(lambda g: quantise("q", g), s - 2)
-            on_group(turn_x, s + 2, 0)
-            on_group(turn_x, s + 2, 1)
+            on_batch(normalise, s - 6)
+            on_group(quantise_q, s - 2)
+            on_pair(turn_x, s + 2, 0)
+            on_pair(turn_x, s + 2, 1)
             on_group(project, s, 2)
             on_group(project, s, 3)
-            on_group(turn_k, s + 2, 0)
-            on_group(turn_k, s + 2, 1)
+            on_pair(turn_k, s + 3, 0)
+            on_pair(turn_k, s + 3, 1)
             on_batch(pick_scores, s - 3)
             on_group(score, s - 2)
             on_group(interleave, s - 1)
-            on_group(widen, s + 3, 0)
+            on_pair(widen, s + 3, 0)
             on_batch(row_max, s - 3)
-            on_batch(row_sum, s - 4)
-            on_group(widen, s + 3, 1)
+            on_batch(row_sum, s - 5)
+            on_pair(widen, s + 3, 1)
+            if s == -1:
+                quantise_x_and_k(s)
+                quantise(w_codes[:], w_scales[:], w_words[:])
             on_batch(shift, s - 3)
-            on_batch(invert, s - 4)
+            on_batch(invert, s - 5)
             on_group(empty_scores, s - 2)
-            if s + 2 >= 0:
-                on_group(load_x, s + 2 + AHEAD)
-                on_group(load_k, s + 2 + AHEAD)
+            on_group(load_x, s - first_step + AHEAD)
+            on_group(load_k, s - first_step + AHEAD)

@@ -26,6 +26,7 @@ BATCH = P // FRAMES
 RING = 6
 AHEAD = 8
 TAIL = 4
+SCALAR_PART = 8
 SOFTMAX_SCALE = 0.125
 
 FLOPS = 2 * TILES * P * D * D + 2 * TILES * P * FRAMES * D
@@ -190,7 +191,9 @@ def tile_dividedspacetimeattention_pa_t_kernel(tc, x_bytes, x_scale, Wq, bq, k, 
             src = planes[g][:].rearrange("p (t n) -> p n t", t=PACK)
             if g + TAIL < n_groups:
                 q_words[g] = work.tile([P, PACK * width], BF16, name="q_words", tag="q_words", bufs=1, align_bytes=64)
-                gpsimd_copy(q_words[g][:].rearrange("p (n t) -> p n t", t=PACK), src)
+                dst = q_words[g][:].rearrange("p (n t) -> p n t", t=PACK)
+                gpsimd_copy(dst[:, width // SCALAR_PART :], src[:, width // SCALAR_PART :])
+                nc.scalar.copy(out=dst[:, : width // SCALAR_PART], in_=src[:, : width // SCALAR_PART])
             else:
                 q_words[g] = work.tile([P, PACK * width], BF16, name="q_words_tail", tag="q_words_tail", align_bytes=64)
                 dst = q_words[g][:].rearrange("p (n t) -> p n t", t=PACK)
@@ -228,7 +231,7 @@ def tile_dividedspacetimeattention_pa_t_kernel(tc, x_bytes, x_scale, Wq, bq, k, 
             slot = r0 - batch_first[b]
             dst = scored[b][:].rearrange("p (c r f) -> p r c f", c=SETS, f=FRAMES)[:, slot : slot + n]
             src = score_bank[g][:, : n * P].rearrange("p (r c f) -> p r c f", c=SETS, f=FRAMES)
-            if g % 2 == 0:
+            if g + TAIL < n_groups:
                 nc.vector.tensor_copy(out=dst, in_=src)
             else:
                 nc.scalar.copy(out=dst, in_=src)
@@ -299,7 +302,6 @@ def tile_dividedspacetimeattention_pa_t_kernel(tc, x_bytes, x_scale, Wq, bq, k, 
             on_group(project, s, 0)
             on_group(project, s, 1)
             on_batch(exponent, s - 4)
-            on_batch(normalise, s - 6)
             on_group(quantise_q, s - 2)
             on_pair(turn_x, s + 2, 0)
             on_pair(turn_x, s + 2, 1)
@@ -311,14 +313,15 @@ def tile_dividedspacetimeattention_pa_t_kernel(tc, x_bytes, x_scale, Wq, bq, k, 
             on_group(score, s - 2)
             on_group(interleave, s - 1)
             on_pair(widen, s + 3, 0)
-            on_batch(row_max, s - 3)
             on_batch(row_sum, s - 5)
             on_pair(widen, s + 3, 1)
             if s == -1:
                 quantise_x_and_k(s)
                 quantise(w_codes[:], w_scales[:], w_words[:])
-            on_batch(shift, s - 3)
+            on_batch(row_max, s - 3)
             on_batch(invert, s - 5)
+            on_batch(shift, s - 3)
             on_group(empty_scores, s - 2)
+            on_batch(normalise, s - 6)
             on_group(load_x, s - first_step + AHEAD)
             on_group(load_k, s - first_step + AHEAD)

from contextlib import ExitStack

import concourse.mybir as mybir
from concourse.masks import make_identity

F32 = mybir.dt.float32
BF16 = mybir.dt.bfloat16
U32 = mybir.dt.uint32
U8 = mybir.dt.uint8
FP8 = mybir.dt.float8_e4m3fn
FP8X4 = mybir.dt.float8_e4m3fn_x4
ALU = mybir.AluOpType
ACT = mybir.ActivationFunctionType
AXIS = mybir.AxisListType

P = 128
D = 512
PACK = 4
FRAMES = 16
SETS = 8
TILES = 98
BANK = 512
PAIR = 2
GROUP = 4
BATCH = P // FRAMES
RING = 6
AHEAD = 8
TAIL = 4
SCALAR_PART = 8
SOFTMAX_SCALE = 0.125

FLOPS = 2 * TILES * P * D * D + 2 * TILES * P * FRAMES * D


def tile_dividedspacetimeattention_pa_t_kernel(tc, x_bytes, x_scale, Wq, bq, k, out):
    nc = tc.nc

    groups = [(0, PAIR)] + [(r0, GROUP) for r0 in range(PAIR, TILES - GROUP, GROUP)]
    groups = groups + [(TILES - GROUP, PAIR), (TILES - PAIR, PAIR)]
    n_groups = len(groups)
    batch_first = [0] + list(range(PAIR, TILES, BATCH))
    batch_rows = [PAIR * FRAMES] + [P] * (len(batch_first) - 1)
    batch_of = [max(b for b, first in enumerate(batch_first) if first <= r0) for r0, n in groups]
    batch_closed_by = {g: b for g, b in enumerate(batch_of) if g + 1 == n_groups or batch_of[g + 1] != b}

    x_rows = x_bytes.rearrange("b (q r) d -> (b q) (r d)", r=TILES)
    k_rows = k.rearrange("b h (j r) g d -> r g (b h j) d", r=TILES)
    out_rows = out.rearrange("b h (j r) f g -> (r f) (b h j) g", r=TILES)

    with ExitStack() as ctx:
        const = ctx.enter_context(tc.tile_pool(name="const", bufs=1))
        loads = ctx.enter_context(tc.tile_pool(name="loads", bufs=1))
        work = ctx.enter_context(tc.tile_pool(name="work", bufs=2))
        psum = ctx.enter_context(tc.psum_pool(name="psum", bufs=1))
        ctx.enter_context(tc.manual_schedule())

        xbytes, kraw, widened, joint, planes, q_words, mx, score_bank, scored, soft = [{} for i in range(10)]

        def load_x(g):
            r0, n = groups[g]
            xbytes[g] = loads.tile([P, n * D], U8, name="xbytes", tag="xbytes", bufs=AHEAD + 2, align_bytes=256)
            nc.sync.dma_start(out=xbytes[g][:], in_=x_rows[:, r0 * D : (r0 + n) * D])

        def load_k(g):
            r0, n = groups[g]
            for h in range(n // PAIR):
                kraw[g, h] = loads.tile([P, PAIR * D], BF16, name="kraw", tag="kraw", bufs=2 * AHEAD, align_bytes=256)
                for i in range(PAIR):
                    nc.sync.dma_start(out=kraw[g, h][:, i * D : (i + 1) * D], in_=k_rows[r0 + PAIR * h + i])

        scale_col = const.tile([P, PACK], F32, name="scale_col")
        nc.sync.dma_start(out=scale_col[:], in_=x_scale.rearrange("a b (p t) -> p (a b t)", t=PACK))
        for g in range(2):
            load_x(g)
            load_k(g)
        w_raw = const.tile([P, PACK, D], BF16, name="w_raw", align_bytes=256)
        nc.sync.dma_start(out=w_raw[:], in_=Wq.rearrange("(p j) c -> p j c", j=PACK))
        bias = const.tile([P, PACK], BF16, name="bias")
        nc.sync.dma_start(out=bias[:], in_=bq.rearrange("(p t) -> p t", t=PACK))
        for g in range(2, AHEAD):
            load_x(g)
            load_k(g)

        def new_scored(b):
            scored[b] = work.tile([P, SETS * P], F32, name="scored", tag="scored")

        new_scored(0)
        nc.vector.memset(scored[0][:].rearrange("p (c r f) -> p c r f", c=SETS, f=FRAMES)[:, :, PAIR:, :], 0.0)

        ident = const.tile([P, P], F32, name="ident")
        make_identity(nc, ident[:])
        x_order = const.tile([P, P], F32, name="x_order")
        nc.vector.tensor_copy(
            out=x_order[:].rearrange("p (b j f) -> p b j f", j=2, f=FRAMES),
            in_=ident[:].rearrange("p (b f j) -> p b j f", j=2, f=FRAMES),
        )
        pick = const.tile([P, 2 * P - FRAMES], F32, name="pick")
        ident_cg = ident[:].rearrange("p (g c) -> p c g", c=SETS)
        nc.vector.tensor_copy(out=pick[:, :P].rearrange("p (c g) -> p c g", g=FRAMES), in_=ident_cg)
        nc.vector.tensor_copy(out=pick[:, P:].rearrange("p (c g) -> p c g", g=FRAMES), in_=ident_cg[:, : SETS - 1, :])

        scales = psum.tile([P, BANK], F32, name="scales", tag="scales")
        for t in range(PACK):
            nc.tensor.transpose(scales[:, t:BANK:PACK], scale_col[:, t : t + 1].to_broadcast([P, P]), ident[:])

        def gpsimd_copy(dst, src):
            nc.gpsimd.tensor_scalar(out=dst, in0=src, scalar1=1.0, scalar2=0.0, op0=ALU.mult, op1=ALU.add)

        w_words = const.tile([P, PACK * D], BF16, name="w_words", align_bytes=64)
        gpsimd_copy(
            w_words[:].rearrange("p (t m j) -> p t m j", t=PACK, j=PACK),
            w_raw[:].rearrange("p j (m t) -> p t m j", t=PACK),
        )
        w_codes = const.tile([P, D], U32, name="w_codes", align_bytes=64)
        w_scales = const.tile([P, D], U8, name="w_scales", align_bytes=64)

        def new_bank():
            return psum.tile([P, BANK], F32, name="bank", tag="bank", bufs=RING)

        def quantise(codes, block_scales, values):
            nc.vector.quantize_mx(out=codes.bitcast(FP8X4), scales=block_scales, in_=values)

        def widen(g, h):
            widened[g, h] = work.tile([P, PAIR * D], BF16, name="widened", tag="widened", bufs=4)
            for r in range(PAIR):
                first = (h * PAIR + r) * D
                nc.vector.tensor_tensor(
                    out=widened[g, h][:, r * D : (r + 1) * D],
                    in0=xbytes[g][:, first : first + D].bitcast(FP8),
                    in1=scales[:],
                    op=ALU.mult,
                )

        def turn(rows, order, step, first):
            bank = new_bank()
            words = rows[:].bitcast(F32)
            for r in range(PAIR):
                for u in range(2):
                    slot = (r * 2 + u) * P
                    nc.tensor.transpose(bank[:, slot : slot + P], words[:, r * 2 * P + u : (r + 1) * 2 * P : 2], order[:])
            if step not in joint:
                joint[step] = work.tile([P, 2 * GROUP * D], BF16, name="joint", tag="joint", bufs=5, align_bytes=64)
            nc.scalar.copy(
                out=joint[step][:, first : first + PAIR * D].bitcast(F32).rearrange("p (r n u) -> p r n u", r=PAIR, u=2),
                in_=bank[:].rearrange("p (r u n) -> p r n u", r=PAIR, u=2),
            )

        def turn_x(g, h):
            turn(widened[g, h], x_order, g - 1, h * PAIR * D)

        def turn_k(g, h):
            turn(kraw[g, h], ident, g + 1, (GROUP + h * PAIR) * D)

        def quantise_x_and_k(step):
            codes = work.tile([P, 2 * BANK], U32, name="xk_codes", tag="xk_codes", align_bytes=64)
            block_scales = work.tile([P, 2 * BANK], U8, name="xk_scales", tag="xk_scales", align_bytes=64)
            parts = [("x", step + 1, 0), ("k", step - 1, BANK)]
            parts = [(name, g, slice(c0, c0 + groups[g][1] * P)) for name, g, c0 in parts if 0 <= g < n_groups]
            for name, g, cols in parts:
                mx[name, g] = (codes[:, cols], block_scales[:, cols])
            if sum(cols.stop - cols.start for name, g, cols in parts) == 2 * BANK:
                quantise(codes[:], block_scales[:], joint[step][:])
            else:
                for name, g, cols in parts:
                    quantise(codes[:, cols], block_scales[:, cols], joint[step][:, PACK * cols.start : PACK * cols.stop])

        def project(g, t):
            width = groups[g][1] * P
            if t == 0:
                planes[g] = work.tile([P, PACK * width], BF16, name="planes", tag="planes", bufs=3)
            x_codes, x_scales = mx["x", g]
            bank = new_bank()
            nc.tensor.matmul_mx(
                out=bank[:, :width],
                lhsT=w_codes[:, t * P : (t + 1) * P].bitcast(FP8X4),
                lhsT_scale=w_scales[:, t * P : (t + 1) * P],
                rhs=x_codes.bitcast(FP8X4),
                rhs_scale=x_scales,
                start=True,
                stop=True,
            )
            nc.scalar.activation(
                out=planes[g][:, t * width : (t + 1) * width],
                in_=bank[:, :width],
                func=ACT.Identity,
                bias=bias[:, t : t + 1],
            )

        def interleave(g):
            width = groups[g][1] * P
            src = planes[g][:].rearrange("p (t n) -> p n t", t=PACK)
            if g + TAIL < n_groups:
                q_words[g] = work.tile([P, PACK * width], BF16, name="q_words", tag="q_words", bufs=1, align_bytes=64)
                dst = q_words[g][:].rearrange("p (n t) -> p n t", t=PACK)
                gpsimd_copy(dst[:, width // SCALAR_PART :], src[:, width // SCALAR_PART :])
                nc.scalar.copy(out=dst[:, : width // SCALAR_PART], in_=src[:, : width // SCALAR_PART])
            else:
                q_words[g] = work.tile([P, PACK * width], BF16, name="q_words_tail", tag="q_words_tail", align_bytes=64)
                dst = q_words[g][:].rearrange("p (n t) -> p n t", t=PACK)
                nc.scalar.copy(out=dst[:, : width // 2], in_=src[:, : width // 2])
                nc.vector.tensor_copy(out=dst[:, width // 2 :], in_=src[:, width // 2 :])

        def quantise_q(g):
            width = groups[g][1] * P
            codes = work.tile([P, width], U32, name="q_codes", tag="q_codes", align_bytes=64)
            block_scales = work.tile([P, width], U8, name="q_scales", tag="q_scales", align_bytes=64)
            quantise(codes[:], block_scales[:], q_words[g][:])
            mx["q", g] = (codes[:], block_scales[:])

        def score(g):
            q_codes, q_scales = mx["q", g]
            k_codes, k_scales = mx["k", g]
            score_bank[g] = new_bank()
            for r in range(groups[g][1]):
                cols = slice(r * P, (r + 1) * P)
                nc.tensor.matmul_mx(
                    out=score_bank[g][:, cols],
                    lhsT=k_codes[:, cols].bitcast(FP8X4),
                    lhsT_scale=k_scales[:, cols],
                    rhs=q_codes[:, cols].bitcast(FP8X4),
                    rhs_scale=q_scales[:, cols],
                    start=True,
                    stop=True,
                )

        def empty_scores(g):
            r0, n = groups[g]
            b = batch_of[g]
            if b not in scored:
                new_scored(b)
            slot = r0 - batch_first[b]
            dst = scored[b][:].rearrange("p (c r f) -> p r c f", c=SETS, f=FRAMES)[:, slot : slot + n]
            src = score_bank[g][:, : n * P].rearrange("p (r c f) -> p r c f", c=SETS, f=FRAMES)
            if g + TAIL < n_groups:
                nc.vector.tensor_copy(out=dst, in_=src)
            else:
                nc.scalar.copy(out=dst, in_=src)

        def by_set(ap):
            return ap.rearrange("p (c g) -> p c g", g=FRAMES)

        def pick_scores(b):
            picked = psum.tile([P, BANK], F32, name="picked", tag="picked")
            for c in range(SETS):
                window = slice(c * FRAMES, c * FRAMES + P)
                nc.tensor.transpose(picked[:, window], scored[b][:, c * P : (c + 1) * P], pick[:, window])
            soft[b, "picked"] = by_set(picked[: batch_rows[b], :P])

        def per_set(ap, b):
            return ap.unsqueeze(2).to_broadcast([batch_rows[b], SETS, FRAMES])

        def row_max(b):
            top = work.tile([P, SETS], F32, name="top", tag="top")
            soft[b, "top"] = top[: batch_rows[b]]
            nc.vector.tensor_reduce(out=soft[b, "top"], in_=soft[b, "picked"], axis=AXIS.X, op=ALU.max)

        def shift(b):
            shifted = work.tile([P, P], F32, name="shifted", tag="shifted")
            soft[b, "shifted"] = shifted[: batch_rows[b]]
            nc.vector.tensor_tensor(
                out=by_set(soft[b, "shifted"]), in0=soft[b, "picked"], in1=per_set(soft[b, "top"], b), op=ALU.subtract
            )

        def exponent(b):
            powers = work.tile([P, P], F32, name="powers", tag="powers")
            soft[b, "powers"] = powers[: batch_rows[b]]
            nc.scalar.activation(out=soft[b, "powers"], in_=soft[b, "shifted"], func=ACT.Exp, scale=SOFTMAX_SCALE)

        def row_sum(b):
            total = work.tile([P, SETS], F32, name="total", tag="total")
            soft[b, "total"] = total[: batch_rows[b]]
            nc.vector.tensor_reduce(out=soft[b, "total"], in_=by_set(soft[b, "powers"]), axis=AXIS.X, op=ALU.add)

        def invert(b):
            inverse = work.tile([P, SETS], F32, name="inverse", tag="inverse")
            soft[b, "inverse"] = inverse[: batch_rows[b]]
            nc.vector.reciprocal(out=soft[b, "inverse"], in_=soft[b, "total"])

        def normalise(b):
            weights = work.tile([P, P], F32, name="weights", tag="weights")
            rows = by_set(weights[: batch_rows[b]])
            nc.vector.tensor_tensor(out=rows, in0=by_set(soft[b, "powers"]), in1=per_set(soft[b, "inverse"], b), op=ALU.mult)
            first = batch_first[b] * FRAMES
            nc.sync.dma_start(out=out_rows[first : first + batch_rows[b]], in_=rows)

        def on_group(fn, g, *args):
            if 0 <= g < n_groups:
                fn(g, *args)

        def on_pair(fn, g, h):
            if 0 <= g < n_groups and h * PAIR < groups[g][1]:
                fn(g, h)

        def on_batch(fn, g):
            if g in batch_closed_by:
                fn(batch_closed_by[g])

        first_step = -3
        for s in range(first_step, n_groups + 6):
            if s >= 0 and s in joint:
                quantise_x_and_k(s)
            on_group(project, s, 0)
            on_group(project, s, 1)
            on_batch(exponent, s - 4)
            on_group(quantise_q, s - 2)
            on_pair(turn_x, s + 2, 0)
            on_pair(turn_x, s + 2, 1)
            on_group(project, s, 2)
            on_group(project, s, 3)
            on_pair(turn_k, s + 3, 0)
            on_pair(turn_k, s + 3, 1)
            on_batch(pick_scores, s - 3)
            on_group(score, s - 2)
            on_group(interleave, s - 1)
            on_pair(widen, s + 3, 0)
            on_batch(row_sum, s - 5)
            on_pair(widen, s + 3, 1)
            if s == -1:
                quantise_x_and_k(s)
                quantise(w_codes[:], w_scales[:], w_words[:])
            on_batch(row_max, s - 3)
            on_batch(invert, s - 5)
            on_batch(shift, s - 3)
            on_group(empty_scores, s - 2)
            on_batch(normalise, s - 6)
            on_group(load_x, s - first_step + AHEAD)
            on_group(load_k, s - first_step + AHEAD)
